import numpy as np
import ml_dtypes


def mxq(x, axis, fmt="e4m3"):
    dtype, down = {"e4m3": (ml_dtypes.float8_e4m3fn, 7), "e5m2": (ml_dtypes.float8_e5m2, 14)}[fmt]
    v = np.moveaxis(np.asarray(x, np.float32).astype(ml_dtypes.bfloat16).astype(np.float64), axis, -1)
    blocks = v.reshape(v.shape[:-1] + (-1, 32))
    amax = np.abs(blocks).max(-1, keepdims=True)
    byte = np.maximum(np.where(amax > 0, np.frexp(amax)[1] - 1 + 127, 0) - down, 1)
    scale = np.exp2(byte - 127.0)
    codes = (blocks / scale).astype(np.float32).astype(dtype).astype(np.float64)
    return np.moveaxis((codes * scale).reshape(v.shape), -1, axis)


WIDE = False


def mx_kscale(k):
    if not WIDE:
        return np.ones(k)
    levels = np.array([10, -10, 5, -5, 0])
    a = np.random.permutation(np.resize(levels, k // 512 * 4)).reshape(k // 512, 4)
    idx = np.arange(k)
    return np.exp2(a[idx // 512, idx % 128 // 32])


BF16 = ml_dtypes.bfloat16


def bf(x):
    return np.asarray(x, np.float32).astype(BF16)


def f64(x):
    return np.asarray(x).astype(np.float64)


E2M1 = np.array([0.0, 0.5, 1.0, 1.5, 2.0, 3.0, 4.0, 6.0, -0.0, -0.5, -1.0, -1.5, -2.0, -3.0, -4.0, -6.0])


def pack_weight(w, fmt):
    k, n = w.shape
    w = f64(bf(w)).reshape(k // 32, 32, n)
    amax = np.abs(w).max(1)
    if fmt == "e4m3":
        byte = np.frexp(amax)[1] - 1 + 127 - 7
    else:
        mant, ex = np.frexp(amax / 6.0)
        byte = np.where(mant > 0.5, ex, ex - 1) + 127
    byte = np.clip(np.where(amax > 0, byte, 1), 1, 254)
    scaled = (w * np.exp2(127.0 - byte)[:, None, :]).reshape(k, n).astype(np.float32)
    by_word = np.ascontiguousarray(scaled.reshape(k // 512, 128, 4, n).transpose(0, 1, 3, 2))
    if fmt == "e4m3":
        words = by_word.astype(ml_dtypes.float8_e4m3fn).view(np.uint8)
    else:
        c = by_word.astype(ml_dtypes.float4_e2m1fn).view(np.uint8) & 0xF
        words = c[..., 0::2] | (c[..., 1::2] << 4)
    return np.ascontiguousarray(words), np.ascontiguousarray(byte.astype(np.uint8).reshape(k // 512, 16, n))


def unpack_weight(words, scales, fmt):
    g, p, n, _ = words.shape
    if fmt == "e4m3":
        vals = np.ascontiguousarray(words).view(ml_dtypes.float8_e4m3fn).astype(np.float64)
    else:
        nib = np.empty((g, p, n, 4), np.uint8)
        nib[..., 0::2] = words & 0xF
        nib[..., 1::2] = words >> 4
        vals = E2M1[nib]
    vals = vals * np.repeat(np.exp2(scales.astype(np.float64) - 127.0), 8, axis=1)[..., None]
    return vals.transpose(0, 1, 3, 2).reshape(g * 512, n)


N, D_IN, H0, H1, K = 256, 16384, 1024, 256, 20
V = 1.0
FMT = "e4m3"


def silu(v):
    return v / (1.0 + np.exp(-v))


def setup_inputs():
    s = mx_kscale(D_IN)
    w1 = np.random.standard_normal((D_IN, H0)) / np.sqrt(D_IN)
    b1 = np.random.standard_normal(H0) * 0.2
    w2 = np.random.standard_normal((H0, H1)) * 4.0 / np.sqrt(H0 * H1)
    b2 = np.random.standard_normal(H1) * 0.1
    cent = np.random.standard_normal((K, D_IN)) * 0.9
    x = cent[np.random.randint(0, K, N)] + np.random.standard_normal((N, D_IN)) * 0.44
    hc = silu(np.stack([(c[:, None] * w1).sum(0) for c in cent]) + b1)
    clusters = (hc[:, :, None] * w2[None]).sum(1) + b2 + np.random.standard_normal((K, H1)) * 0.5 / np.sqrt(H1)
    W1_words, W1_scales = pack_weight(w1 / s[:, None], FMT)
    W2_words, W2_scales = pack_weight(w2, FMT)
    return {"x": bf(x * s), "W1_words": W1_words, "W1_scales": W1_scales, "b1": bf(b1), "W2_words": W2_words, "W2_scales": W2_scales, "b2": bf(b2), "clusters": bf(clusters)}


def reference(x, W1_words, W1_scales, b1, W2_words, W2_scales, b2, clusters):
    h = silu((mxq(f64(x), 1, "e4m3") @ unpack_weight(W1_words, W1_scales, FMT)) + f64(b1))
    z = (mxq(h, 1, "e4m3") @ unpack_weight(W2_words, W2_scales, FMT)) + f64(b2)
    d2 = np.stack([((z - c) ** 2).sum(1) for c in f64(clusters)], axis=1)
    q = 1.0 / (1.0 + d2 / V)
    q = q ** ((V + 1.0) / 2.0)
    q = q / q.sum(1, keepdims=True)
    return z, q

@@ -1,0 +1,302 @@
+from contextlib import ExitStack
+
+import concourse.mybir as mybir
+from concourse.masks import make_identity
+
+F32 = mybir.dt.float32
+BF16 = mybir.dt.bfloat16
+I32 = mybir.dt.int32
+U32 = mybir.dt.uint32
+U8 = mybir.dt.uint8
+FP8X4 = mybir.dt.float8_e4m3fn_x4
+ACT = mybir.ActivationFunctionType
+ALU = mybir.AluOpType
+AXIS = mybir.AxisListType
+
+P = 128
+PACK = 4
+K_PASS = P * PACK
+ROWS = 256
+ROW_TILES = ROWS // P
+D_IN = 16384
+H0 = 1024
+H1 = 256
+CENTROIDS = 20
+GROUPS1 = D_IN // K_PASS
+GROUPS2 = H0 // K_PASS
+N_TILE = 512
+HALVES = H0 // N_TILE
+J_TILES = H1 // P
+BLOCK = 4
+BLOCKS = GROUPS1 // BLOCK
+WORDS = K_PASS // 2
+W1_BUFS = 14
+
+FLOPS = 2 * ROWS * D_IN * H0 + 2 * ROWS * H0 * H1 + 3 * ROWS * CENTROIDS * H1
+
+
+def tile_lintrans_pa_k_kernel(
+    tc, x, W1_words, W1_scales, b1, W2_words, W2_scales, b2, clusters, out_0, out_1
+):
+    nc = tc.nc
+    with ExitStack() as stack:
+        stack.enter_context(tc.manual_schedule())
+        keep = stack.enter_context(tc.tile_pool(name="keep", bufs=1))
+        x_pool = stack.enter_context(tc.tile_pool(name="x_pool", bufs=BLOCKS))
+        grouped_pool = stack.enter_context(tc.tile_pool(name="grouped_pool", bufs=3))
+        w1_pool = stack.enter_context(tc.tile_pool(name="w1_pool", bufs=W1_BUFS))
+        pre_pool = stack.enter_context(tc.tile_pool(name="pre_pool", bufs=4))
+        acc_pool = stack.enter_context(tc.psum_pool(name="acc_pool", bufs=1))
+        work_pool = stack.enter_context(tc.psum_pool(name="work_pool", bufs=4))
+
+        bias_rows = keep.tile([P, H0 + H1], BF16)
+        nc.vector.memset(bias_rows[:], 0.0)
+        cl_bf = keep.tile([P, H1], BF16)
+        nc.vector.memset(cl_bf[:], 0.0)
+        silu_in = keep.tile([P, 1], F32)
+        nc.vector.memset(silu_in[:], 0.0)
+        w1_planes = keep.tile([P, BLOCKS, H0], U8, align_bytes=64)
+        nc.vector.memset(w1_planes[:].bitcast(I32), 0)
+        w2_planes = keep.tile([P, GROUPS2, H1], U8, align_bytes=64)
+        nc.vector.memset(w2_planes[:].bitcast(I32), 0)
+        ones_bf = keep.tile([P, P], BF16)
+        nc.vector.memset(ones_bf[:], 1.0)
+        ones_f32 = keep.tile([P, P], F32)
+        nc.vector.memset(ones_f32[:], 1.0)
+        ident = keep.tile([P, P], F32)
+        make_identity(nc, ident[:])
+
+        nc.scalar.dma_start(out=bias_rows[0:1, 0:H0], in_=b1.unsqueeze(0))
+        nc.scalar.dma_start(out=bias_rows[0:1, H0 : H0 + H1], in_=b2.unsqueeze(0))
+        nc.scalar.dma_start(out=cl_bf[0:CENTROIDS, :], in_=clusters)
+        nc.scalar.dma_start(out=cl_bf[CENTROIDS : CENTROIDS + 1, :], in_=b2.unsqueeze(0))
+        silu_out = keep.tile([P, 1], F32)
+        nc.scalar.activation(out=silu_out[:], in_=silu_in[:], func=ACT.Silu)
+
+        x_view = x.rearrange("(p e) k -> p e k", e=ROW_TILES)
+        x_raw = []
+        for b in range(BLOCKS):
+            x_block = x_pool.tile([P, ROW_TILES, BLOCK * K_PASS], BF16, name="x_block")
+            k_cols = slice(b * BLOCK * K_PASS, (b + 1) * BLOCK * K_PASS)
+            nc.sync.dma_start(out=x_block[:], in_=x_view[:, :, k_cols])
+            x_raw.append(x_block)
+
+        for b in range(BLOCKS):
+            for quad in range(4):
+                nc.sync.dma_start(
+                    out=w1_planes[32 * quad : 32 * quad + 16, b, :].bitcast(I32),
+                    in_=W1_scales[b * BLOCK : (b + 1) * BLOCK, 4 * quad : 4 * quad + 4, :].bitcast(I32),
+                )
+        for quad in range(4):
+            nc.sync.dma_start(
+                out=w2_planes[32 * quad : 32 * quad + 4, :, :].bitcast(I32),
+                in_=W2_scales[:, 4 * quad : 4 * quad + 4, :].rearrange("g r n -> r g n").bitcast(I32),
+            )
+        w2_words = keep.tile([P, GROUPS2, H1], U32, align_bytes=64)
+        nc.sync.dma_start(
+            out=w2_words[:].bitcast(I32),
+            in_=W2_words.rearrange("g p n t -> p g (n t)").bitcast(I32),
+        )
+
+        w1_view = W1_words.rearrange("g p n t -> g p (n t)").bitcast(I32)
+
+        def load_w1(g):
+            w1_group = w1_pool.tile([P, H0], U32, name="w1_group", align_bytes=64)
+            nc.sync.dma_start(out=w1_group[:].bitcast(I32), in_=w1_view[g])
+            return w1_group
+
+        w1_tiles = [load_w1(g) for g in range(W1_BUFS)]
+
+        x_codes = keep.tile([P, GROUPS1, ROWS], U32, align_bytes=64)
+        x_planes = keep.tile([P, GROUPS1, ROWS], U8, align_bytes=64)
+
+        def transpose_block(b):
+            grouped = grouped_pool.tile([P, BLOCK, ROWS, PACK], BF16, name="grouped", align_bytes=64)
+            x_words = x_raw[b][:].bitcast(F32)
+            for i in range(BLOCK):
+                xt = work_pool.tile([P, 2, ROWS], F32, name="xt", tag="work")
+                for u in range(2):
+                    for e in range(ROW_TILES):
+                        nc.tensor.transpose(
+                            xt[:, u, e * P : (e + 1) * P],
+                            x_words[:, e, WORDS * i + u : WORDS * (i + 1) : 2],
+                            ident[:],
+                        )
+                dst = grouped[:, i, :, :].bitcast(F32)
+                src = xt[:].rearrange("p u r -> p r u")
+                if i == BLOCK - 1:
+                    nc.vector.tensor_copy(out=dst, in_=src)
+                else:
+                    nc.scalar.copy(out=dst, in_=src)
+            return grouped
+
+        def quantise_block(b, grouped):
+            groups = slice(b * BLOCK, (b + 1) * BLOCK)
+            nc.vector.quantize_mx(
+                out=x_codes[:, groups, :].rearrange("p g r -> p (g r)").bitcast(FP8X4),
+                scales=x_planes[:, groups, :].rearrange("p g r -> p (g r)"),
+                in_=grouped[:].rearrange("p g r t -> p (g r t)"),
+            )
+
+        waiting = transpose_block(0)
+        for b in range(1, BLOCKS):
+            fresh = transpose_block(b)
+            quantise_block(b - 1, waiting)
+            waiting = fresh
+        quantise_block(BLOCKS - 1, waiting)
+
+        b1_sorted = keep.tile([P, GROUPS2, PACK, P], F32)
+        for g2 in range(GROUPS2):
+            b1_ps = work_pool.tile([P, K_PASS], F32, name="b1_ps", tag="work")
+            nc.tensor.matmul(
+                b1_ps[:], lhsT=ones_bf[:], rhs=bias_rows[:, g2 * K_PASS : (g2 + 1) * K_PASS], start=True, stop=True
+            )
+            nc.vector.tensor_copy(out=b1_sorted[:, g2, :, :], in_=b1_ps[:].rearrange("r (p t) -> r t p", t=PACK))
+        b2_ps = work_pool.tile([P, H1], F32, name="b2_ps", tag="work")
+        nc.tensor.matmul(b2_ps[:], lhsT=ones_bf[:], rhs=bias_rows[:, H0 : H0 + H1], start=True, stop=True)
+        b2_rows = keep.tile([P, H1], F32)
+        nc.vector.tensor_copy(out=b2_rows[:], in_=b2_ps[:])
+
+        cl_f32 = keep.tile([P, H1], F32)
+        nc.vector.tensor_copy(out=cl_f32[:], in_=cl_bf[:])
+        clT_ps = work_pool.tile([P, J_TILES, P], F32, name="clT_ps", tag="work")
+        for jt in range(J_TILES):
+            nc.tensor.transpose(clT_ps[:, jt, :], cl_f32[:, jt * P : (jt + 1) * P], ident[:])
+        clT = keep.tile([P, J_TILES, 32], F32)
+        nc.vector.tensor_copy(out=clT[:], in_=clT_ps[:, :, 0:32])
+        c_m2 = keep.tile([P, J_TILES, CENTROIDS], F32)
+        nc.vector.tensor_scalar_mul(out=c_m2[:], in0=clT[:, :, 0:CENTROIDS], scalar1=-2.0)
+        c_sq = keep.tile([P, J_TILES, CENTROIDS], F32)
+        nc.vector.tensor_mul(out=c_sq[:], in0=clT[:, :, 0:CENTROIDS], in1=clT[:, :, 0:CENTROIDS])
+        cc_ps = work_pool.tile([P, CENTROIDS], F32, name="cc_ps", tag="work")
+        for jt in range(J_TILES):
+            nc.tensor.matmul(
+                cc_ps[:], lhsT=ones_f32[:], rhs=c_sq[:, jt, :], start=(jt == 0), stop=(jt == J_TILES - 1)
+            )
+        cc1 = keep.tile([P, CENTROIDS], F32)
+        nc.vector.tensor_scalar_add(out=cc1[:], in0=cc_ps[:], scalar1=1.0)
+
+        acc = {}
+        for half in range(HALVES):
+            for e in range(ROW_TILES):
+                acc[(e, half)] = acc_pool.tile([P, N_TILE], F32, name="acc_%d%d" % (e, half))
+        for g in range(GROUPS1):
+            b, i = divmod(g, BLOCK)
+            for half in range(HALVES):
+                cols = slice(half * N_TILE, (half + 1) * N_TILE)
+                for e in range(ROW_TILES):
+                    rows = slice(e * P, (e + 1) * P)
+                    nc.tensor.matmul_mx(
+                        out=acc[(e, half)][:],
+                        lhsT=x_codes[:, g, rows].bitcast(FP8X4),
+                        lhsT_scale=x_planes[:, g, rows],
+                        rhs=w1_tiles[g][:, cols].bitcast(FP8X4),
+                        rhs_scale=w1_planes[PACK * i : P, b, cols],
+                        start=(g == 0),
+                        stop=(g == GROUPS1 - 1),
+                    )
+            if g + W1_BUFS < GROUPS1:
+                w1_tiles.append(load_w1(g + W1_BUFS))
+
+        h_grouped = keep.tile([P, GROUPS2, ROWS, PACK], BF16, align_bytes=64)
+        h_codes = keep.tile([P, GROUPS2, ROWS], U32, align_bytes=64)
+        h_planes = keep.tile([P, GROUPS2, ROWS], U8, align_bytes=64)
+        for g2 in range(GROUPS2):
+            for e in range(ROW_TILES):
+                pre = pre_pool.tile([P, PACK, P], F32, name="pre")
+                nc.vector.tensor_tensor(
+                    out=pre[:],
+                    in0=acc[(e, g2)][:].rearrange("r (p t) -> r t p", t=PACK),
+                    in1=b1_sorted[:, g2, :, :],
+                    op=ALU.add,
+                )
+                preT = work_pool.tile([P, PACK, P], F32, name="preT", tag="work")
+                for t in range(PACK):
+                    nc.tensor.transpose(preT[:, t, :], pre[:, t, :], ident[:])
+                nc.scalar.activation(
+                    out=h_grouped[:, g2, e * P : (e + 1) * P, :],
+                    in_=preT[:].rearrange("p t r -> p r t"),
+                    func=ACT.Silu,
+                )
+        for g2 in range(GROUPS2):
+            nc.vector.quantize_mx(
+                out=h_codes[:, g2, :].bitcast(FP8X4),
+                scales=h_planes[:, g2, :],
+                in_=h_grouped[:, g2, :, :].rearrange("p r t -> p (r t)"),
+            )
+
+        zT_ps = [acc_pool.tile([P, ROWS], F32, name="zT_ps%d" % jt, tag="acc_%d0" % jt) for jt in range(J_TILES)]
+        z_ps = [acc_pool.tile([P, H1], F32, name="z_ps%d" % e, tag="acc_%d1" % e) for e in range(ROW_TILES)]
+        for g2 in range(GROUPS2):
+            for jt in range(J_TILES):
+                j_cols = slice(jt * P, (jt + 1) * P)
+                nc.tensor.matmul_mx(
+                    out=zT_ps[jt][:],
+                    lhsT=w2_words[:, g2, j_cols].bitcast(FP8X4),
+                    lhsT_scale=w2_planes[:, g2, j_cols],
+                    rhs=h_codes[:, g2, :].bitcast(FP8X4),
+                    rhs_scale=h_planes[:, g2, :],
+                    start=(g2 == 0),
+                    stop=(g2 == GROUPS2 - 1),
+                )
+            for e in range(ROW_TILES):
+                rows = slice(e * P, (e + 1) * P)
+                nc.tensor.matmul_mx(
+                    out=z_ps[e][:],
+                    lhsT=h_codes[:, g2, rows].bitcast(FP8X4),
+                    lhsT_scale=h_planes[:, g2, rows],
+                    rhs=w2_words[:, g2, :].bitcast(FP8X4),
+                    rhs_scale=w2_planes[:, g2, :],
+                    start=(g2 == 0),
+                    stop=(g2 == GROUPS2 - 1),
+                )
+
+        zT = keep.tile([P, J_TILES, ROWS], F32)
+        nc.scalar.activation(
+            out=zT[:, 0, :], in_=zT_ps[0][:], func=ACT.Identity, bias=clT[:, 0, CENTROIDS : CENTROIDS + 1]
+        )
+        nc.vector.tensor_scalar_add(out=zT[:, 1, :], in0=zT_ps[1][:], scalar1=clT[:, 1, CENTROIDS : CENTROIDS + 1])
+        z = keep.tile([P, ROW_TILES, H1], F32)
+        for e in range(ROW_TILES):
+            nc.vector.tensor_tensor(out=z[:, e, :], in0=z_ps[e][:], in1=b2_rows[:], op=ALU.add)
+        nc.sync.dma_start(out=out_0.rearrange("(p e) j -> p e j", e=ROW_TILES), in_=z[:])
+
+        z_sq = keep.tile([P, ROW_TILES, H1], F32)
+        zz = keep.tile([P, ROW_TILES], F32)
+        for e in range(ROW_TILES):
+            nc.scalar.activation(out=z_sq[:, e, :], in_=z[:, e, :], func=ACT.Square, accum_out=zz[:, e : e + 1])
+
+        dots = work_pool.tile([P, ROW_TILES, 32], F32, name="dots", tag="work")
+        for e in range(ROW_TILES):
+            for jt in range(J_TILES):
+                nc.tensor.matmul(
+                    dots[:, e, 0:CENTROIDS],
+                    lhsT=zT[:, jt, e * P : (e + 1) * P],
+                    rhs=c_m2[:, jt, :],
+                    start=(jt == 0),
+                    stop=(jt == J_TILES - 1),
+                )
+        one_plus_d2 = keep.tile([P, ROW_TILES, CENTROIDS], F32)
+        for e in range(ROW_TILES):
+            nc.vector.scalar_tensor_tensor(
+                out=one_plus_d2[:, e, :],
+                in0=dots[:, e, 0:CENTROIDS],
+                scalar=zz[:, e : e + 1],
+                in1=cc1[:],
+                op0=ALU.add,
+                op1=ALU.add,
+            )
+        kern = keep.tile([P, ROW_TILES, CENTROIDS], F32)
+        nc.vector.reciprocal(out=kern[:], in_=one_plus_d2[:])
+        kern_sum = keep.tile([P, ROW_TILES], F32)
+        nc.vector.tensor_reduce(out=kern_sum[:], in_=kern[:], axis=AXIS.X, op=ALU.add)
+        inv_sum = keep.tile([P, ROW_TILES], F32)
+        nc.vector.reciprocal(out=inv_sum[:], in_=kern_sum[:])
+        q = keep.tile([P, ROW_TILES, CENTROIDS], F32)
+        nc.vector.tensor_tensor(
+            out=q[:],
+            in0=kern[:],
+            in1=inv_sum[:].unsqueeze(2).to_broadcast([P, ROW_TILES, CENTROIDS]),
+            op=ALU.mult,
+        )
+        nc.sync.dma_start(out=out_1.rearrange("(p e) k -> p e k", e=ROW_TILES), in_=q[:])

@@ -69,7 +69,6 @@ def tile_lintrans_pa_k_kernel(
         nc.scalar.dma_start(out=bias_rows[0:1, 0:H0], in_=b1.unsqueeze(0))
         nc.scalar.dma_start(out=bias_rows[0:1, H0 : H0 + H1], in_=b2.unsqueeze(0))
         nc.scalar.dma_start(out=cl_bf[0:CENTROIDS, :], in_=clusters)
-        nc.scalar.dma_start(out=cl_bf[CENTROIDS : CENTROIDS + 1, :], in_=b2.unsqueeze(0))
         silu_out = keep.tile([P, 1], F32)
         nc.scalar.activation(out=silu_out[:], in_=silu_in[:], func=ACT.Silu)
 
@@ -83,14 +82,14 @@ def tile_lintrans_pa_k_kernel(
 
         for b in range(BLOCKS):
             for quad in range(4):
-                nc.sync.dma_start(
-                    out=w1_planes[32 * quad : 32 * quad + 16, b, :].bitcast(I32),
-                    in_=W1_scales[b * BLOCK : (b + 1) * BLOCK, 4 * quad : 4 * quad + 4, :].bitcast(I32),
+                nc.gpsimd.dma_start(
+                    out=w1_planes[32 * quad : 32 * quad + 16, b, :].bitcast(F32),
+                    in_=W1_scales[b * BLOCK : (b + 1) * BLOCK, 4 * quad : 4 * quad + 4, :].bitcast(F32),
                 )
         for quad in range(4):
-            nc.sync.dma_start(
-                out=w2_planes[32 * quad : 32 * quad + 4, :, :].bitcast(I32),
-                in_=W2_scales[:, 4 * quad : 4 * quad + 4, :].rearrange("g r n -> r g n").bitcast(I32),
+            nc.gpsimd.dma_start(
+                out=w2_planes[32 * quad : 32 * quad + 4, :, :].bitcast(F32),
+                in_=W2_scales[:, 4 * quad : 4 * quad + 4, :].rearrange("g r n -> r g n").bitcast(F32),
             )
         w2_words = keep.tile([P, GROUPS2, H1], U32, align_bytes=64)
         nc.sync.dma_start(
@@ -138,48 +137,59 @@ def tile_lintrans_pa_k_kernel(
                 in_=grouped[:].rearrange("p g r t -> p (g r t)"),
             )
 
+        b1_sorted = keep.tile([P, GROUPS2, PACK, P], F32)
+        b2_rows = keep.tile([P, H1], F32)
+        cl_shift = keep.tile([P, H1], F32)
+        c_m2 = keep.tile([P, J_TILES, CENTROIDS], F32)
+        c_sq = keep.tile([P, J_TILES, CENTROIDS], F32)
+        cc1 = keep.tile([P, CENTROIDS], F32)
+
+        def spread_biases():
+            for g2 in range(GROUPS2):
+                b1_ps = acc_pool.tile([P, K_PASS], F32, name="b1_ps", tag="bank_%d" % g2)
+                nc.tensor.matmul(
+                    b1_ps[:], lhsT=ones_bf[:], rhs=bias_rows[:, g2 * K_PASS : (g2 + 1) * K_PASS], start=True, stop=True
+                )
+                nc.vector.tensor_copy(out=b1_sorted[:, g2, :, :], in_=b1_ps[:].rearrange("r (p t) -> r t p", t=PACK))
+            b2_ps = acc_pool.tile([P, H1], F32, name="b2_ps", tag="bank_2")
+            nc.tensor.matmul(b2_ps[:], lhsT=ones_bf[:], rhs=bias_rows[:, H0 : H0 + H1], start=True, stop=True)
+            nc.vector.tensor_copy(out=b2_rows[:], in_=b2_ps[:])
+            nc.vector.tensor_tensor(out=cl_shift[:], in0=cl_bf[:], in1=b2_rows[:], op=ALU.subtract)
+
+        def transpose_centroids():
+            clT_ps = acc_pool.tile([P, J_TILES, P], F32, name="clT_ps", tag="bank_3")
+            for jt in range(J_TILES):
+                nc.tensor.transpose(clT_ps[:, jt, :], cl_shift[:, jt * P : (jt + 1) * P], ident[:])
+            nc.vector.tensor_scalar_mul(out=c_m2[:], in0=clT_ps[:, :, 0:CENTROIDS], scalar1=-2.0)
+            nc.vector.scalar_tensor_tensor(
+                out=c_sq[:], in0=c_m2[:], scalar=0.25, in1=c_m2[:], op0=ALU.mult, op1=ALU.mult
+            )
+
+        def centroid_norms():
+            cc_ps = acc_pool.tile([P, CENTROIDS], F32, name="cc_ps", tag="bank_0")
+            for jt in range(J_TILES):
+                nc.tensor.matmul(
+                    cc_ps[:], lhsT=ones_f32[:], rhs=c_sq[:, jt, :], start=(jt == 0), stop=(jt == J_TILES - 1)
+                )
+            nc.vector.tensor_scalar_add(out=cc1[:], in0=cc_ps[:], scalar1=1.0)
+
+        side_jobs = [spread_biases, transpose_centroids, centroid_norms]
+
         waiting = transpose_block(0)
         for b in range(1, BLOCKS):
             fresh = transpose_block(b)
             quantise_block(b - 1, waiting)
             waiting = fresh
+            if b <= len(side_jobs):
+                side_jobs[b - 1]()
         quantise_block(BLOCKS - 1, waiting)
-
-        b1_sorted = keep.tile([P, GROUPS2, PACK, P], F32)
-        for g2 in range(GROUPS2):
-            b1_ps = work_pool.tile([P, K_PASS], F32, name="b1_ps", tag="work")
-            nc.tensor.matmul(
-                b1_ps[:], lhsT=ones_bf[:], rhs=bias_rows[:, g2 * K_PASS : (g2 + 1) * K_PASS], start=True, stop=True
-            )
-            nc.vector.tensor_copy(out=b1_sorted[:, g2, :, :], in_=b1_ps[:].rearrange("r (p t) -> r t p", t=PACK))
-        b2_ps = work_pool.tile([P, H1], F32, name="b2_ps", tag="work")
-        nc.tensor.matmul(b2_ps[:], lhsT=ones_bf[:], rhs=bias_rows[:, H0 : H0 + H1], start=True, stop=True)
-        b2_rows = keep.tile([P, H1], F32)
-        nc.vector.tensor_copy(out=b2_rows[:], in_=b2_ps[:])
-
-        cl_f32 = keep.tile([P, H1], F32)
-        nc.vector.tensor_copy(out=cl_f32[:], in_=cl_bf[:])
-        clT_ps = work_pool.tile([P, J_TILES, P], F32, name="clT_ps", tag="work")
-        for jt in range(J_TILES):
-            nc.tensor.transpose(clT_ps[:, jt, :], cl_f32[:, jt * P : (jt + 1) * P], ident[:])
-        clT = keep.tile([P, J_TILES, 32], F32)
-        nc.vector.tensor_copy(out=clT[:], in_=clT_ps[:, :, 0:32])
-        c_m2 = keep.tile([P, J_TILES, CENTROIDS], F32)
-        nc.vector.tensor_scalar_mul(out=c_m2[:], in0=clT[:, :, 0:CENTROIDS], scalar1=-2.0)
-        c_sq = keep.tile([P, J_TILES, CENTROIDS], F32)
-        nc.vector.tensor_mul(out=c_sq[:], in0=clT[:, :, 0:CENTROIDS], in1=clT[:, :, 0:CENTROIDS])
-        cc_ps = work_pool.tile([P, CENTROIDS], F32, name="cc_ps", tag="work")
-        for jt in range(J_TILES):
-            nc.tensor.matmul(
-                cc_ps[:], lhsT=ones_f32[:], rhs=c_sq[:, jt, :], start=(jt == 0), stop=(jt == J_TILES - 1)
-            )
-        cc1 = keep.tile([P, CENTROIDS], F32)
-        nc.vector.tensor_scalar_add(out=cc1[:], in0=cc_ps[:], scalar1=1.0)
 
         acc = {}
         for half in range(HALVES):
             for e in range(ROW_TILES):
-                acc[(e, half)] = acc_pool.tile([P, N_TILE], F32, name="acc_%d%d" % (e, half))
+                acc[(e, half)] = acc_pool.tile(
+                    [P, N_TILE], F32, name="acc_%d%d" % (e, half), tag="bank_%d" % (ROW_TILES * half + e)
+                )
         for g in range(GROUPS1):
             b, i = divmod(g, BLOCK)
             for half in range(HALVES):
@@ -225,8 +235,8 @@ def tile_lintrans_pa_k_kernel(
                 in_=h_grouped[:, g2, :, :].rearrange("p r t -> p (r t)"),
             )
 
-        zT_ps = [acc_pool.tile([P, ROWS], F32, name="zT_ps%d" % jt, tag="acc_%d0" % jt) for jt in range(J_TILES)]
-        z_ps = [acc_pool.tile([P, H1], F32, name="z_ps%d" % e, tag="acc_%d1" % e) for e in range(ROW_TILES)]
+        zT_ps = [acc_pool.tile([P, ROWS], F32, name="zT_ps%d" % jt, tag="bank_%d" % jt) for jt in range(J_TILES)]
+        z_ps = [acc_pool.tile([P, H1], F32, name="z_ps%d" % e, tag="bank_%d" % (J_TILES + e)) for e in range(ROW_TILES)]
         for g2 in range(GROUPS2):
             for jt in range(J_TILES):
                 j_cols = slice(jt * P, (jt + 1) * P)
@@ -252,19 +262,16 @@ def tile_lintrans_pa_k_kernel(
                 )
 
         zT = keep.tile([P, J_TILES, ROWS], F32)
-        nc.scalar.activation(
-            out=zT[:, 0, :], in_=zT_ps[0][:], func=ACT.Identity, bias=clT[:, 0, CENTROIDS : CENTROIDS + 1]
-        )
-        nc.vector.tensor_scalar_add(out=zT[:, 1, :], in0=zT_ps[1][:], scalar1=clT[:, 1, CENTROIDS : CENTROIDS + 1])
+        nc.scalar.copy(out=zT[:, 0, :], in_=zT_ps[0][:])
+        nc.vector.tensor_copy(out=zT[:, 1, :], in_=zT_ps[1][:])
+        z_sq = keep.tile([P, ROW_TILES, H1], F32)
+        zz = keep.tile([P, ROW_TILES], F32)
+        for e in range(ROW_TILES):
+            nc.scalar.activation(out=z_sq[:, e, :], in_=z_ps[e][:], func=ACT.Square, accum_out=zz[:, e : e + 1])
         z = keep.tile([P, ROW_TILES, H1], F32)
         for e in range(ROW_TILES):
             nc.vector.tensor_tensor(out=z[:, e, :], in0=z_ps[e][:], in1=b2_rows[:], op=ALU.add)
         nc.sync.dma_start(out=out_0.rearrange("(p e) j -> p e j", e=ROW_TILES), in_=z[:])
-
-        z_sq = keep.tile([P, ROW_TILES, H1], F32)
-        zz = keep.tile([P, ROW_TILES], F32)
-        for e in range(ROW_TILES):
-            nc.scalar.activation(out=z_sq[:, e, :], in_=z[:, e, :], func=ACT.Square, accum_out=zz[:, e : e + 1])
 
         dots = work_pool.tile([P, ROW_TILES, 32], F32, name="dots", tag="work")
         for e in range(ROW_TILES):

@@ -31,6 +31,7 @@ BLOCK = 4
 BLOCKS = GROUPS1 // BLOCK
 WORDS = K_PASS // 2
 W1_BUFS = 14
+X_LEAD = 2
 
 FLOPS = 2 * ROWS * D_IN * H0 + 2 * ROWS * H0 * H1 + 3 * ROWS * CENTROIDS * H1
 
@@ -42,8 +43,9 @@ def tile_lintrans_pa_k_kernel(
     with ExitStack() as stack:
         stack.enter_context(tc.manual_schedule())
         keep = stack.enter_context(tc.tile_pool(name="keep", bufs=1))
-        x_pool = stack.enter_context(tc.tile_pool(name="x_pool", bufs=BLOCKS))
-        grouped_pool = stack.enter_context(tc.tile_pool(name="grouped_pool", bufs=3))
+        x_pool = stack.enter_context(tc.tile_pool(name="x_pool", bufs=X_LEAD + 1))
+        sorted_pool = stack.enter_context(tc.tile_pool(name="sorted_pool", bufs=2))
+        grouped_pool = stack.enter_context(tc.tile_pool(name="grouped_pool", bufs=2))
         w1_pool = stack.enter_context(tc.tile_pool(name="w1_pool", bufs=W1_BUFS))
         pre_pool = stack.enter_context(tc.tile_pool(name="pre_pool", bufs=4))
         acc_pool = stack.enter_context(tc.psum_pool(name="acc_pool", bufs=1))
@@ -72,14 +74,6 @@ def tile_lintrans_pa_k_kernel(
         silu_out = keep.tile([P, 1], F32)
         nc.scalar.activation(out=silu_out[:], in_=silu_in[:], func=ACT.Silu)
 
-        x_view = x.rearrange("(p e) k -> p e k", e=ROW_TILES)
-        x_raw = []
-        for b in range(BLOCKS):
-            x_block = x_pool.tile([P, ROW_TILES, BLOCK * K_PASS], BF16, name="x_block")
-            k_cols = slice(b * BLOCK * K_PASS, (b + 1) * BLOCK * K_PASS)
-            nc.sync.dma_start(out=x_block[:], in_=x_view[:, :, k_cols])
-            x_raw.append(x_block)
-
         for b in range(BLOCKS):
             for quad in range(4):
                 nc.gpsimd.dma_start(
@@ -91,51 +85,81 @@ def tile_lintrans_pa_k_kernel(
                 out=w2_planes[32 * quad : 32 * quad + 4, :, :].bitcast(F32),
                 in_=W2_scales[:, 4 * quad : 4 * quad + 4, :].rearrange("g r n -> r g n").bitcast(F32),
             )
-        w2_words = keep.tile([P, GROUPS2, H1], U32, align_bytes=64)
-        nc.sync.dma_start(
-            out=w2_words[:].bitcast(I32),
-            in_=W2_words.rearrange("g p n t -> p g (n t)").bitcast(I32),
-        )
 
+        x_view = x.rearrange("(p e) k -> p e k", e=ROW_TILES)
         w1_view = W1_words.rearrange("g p n t -> g p (n t)").bitcast(I32)
-
-        def load_w1(g):
-            w1_group = w1_pool.tile([P, H0], U32, name="w1_group", align_bytes=64)
-            nc.sync.dma_start(out=w1_group[:].bitcast(I32), in_=w1_view[g])
-            return w1_group
-
-        w1_tiles = [load_w1(g) for g in range(W1_BUFS)]
-
         x_codes = keep.tile([P, GROUPS1, ROWS], U32, align_bytes=64)
         x_planes = keep.tile([P, GROUPS1, ROWS], U8, align_bytes=64)
+        x_raw = {}
+        x_grouped = {}
+        w1_tiles = {}
+
+        def load_x(b):
+            x_block = x_pool.tile([P, ROW_TILES, BLOCK * K_PASS], BF16, name="x_block")
+            k_cols = slice(b * BLOCK * K_PASS, (b + 1) * BLOCK * K_PASS)
+            nc.sync.dma_start(out=x_block[:], in_=x_view[:, :, k_cols])
+            x_raw[b] = x_block
+
+        def load_w1(b):
+            for g in range(b * BLOCK, (b + 1) * BLOCK):
+                w1_group = w1_pool.tile([P, H0], U32, name="w1_group", align_bytes=64)
+                nc.sync.dma_start(out=w1_group[:].bitcast(I32), in_=w1_view[g])
+                w1_tiles[g] = w1_group
 
         def transpose_block(b):
-            grouped = grouped_pool.tile([P, BLOCK, ROWS, PACK], BF16, name="grouped", align_bytes=64)
+            x_sorted = sorted_pool.tile([P, ROW_TILES, BLOCK, 2, P], F32, name="x_sorted")
             x_words = x_raw[b][:].bitcast(F32)
+            nc.vector.tensor_copy(
+                out=x_sorted[:, 0, :, :, :], in_=x_words[:, 0, :].rearrange("r (i p u) -> r i u p", i=BLOCK, u=2)
+            )
+            nc.scalar.copy(
+                out=x_sorted[:, 1, :, :, :], in_=x_words[:, 1, :].rearrange("r (i p u) -> r i u p", i=BLOCK, u=2)
+            )
+            grouped = grouped_pool.tile([P, BLOCK, ROWS, PACK], BF16, name="grouped", align_bytes=64)
             for i in range(BLOCK):
                 xt = work_pool.tile([P, 2, ROWS], F32, name="xt", tag="work")
                 for u in range(2):
                     for e in range(ROW_TILES):
-                        nc.tensor.transpose(
-                            xt[:, u, e * P : (e + 1) * P],
-                            x_words[:, e, WORDS * i + u : WORDS * (i + 1) : 2],
-                            ident[:],
-                        )
+                        nc.tensor.transpose(xt[:, u, e * P : (e + 1) * P], x_sorted[:, e, i, u, :], ident[:])
                 dst = grouped[:, i, :, :].bitcast(F32)
                 src = xt[:].rearrange("p u r -> p r u")
                 if i == BLOCK - 1:
                     nc.vector.tensor_copy(out=dst, in_=src)
                 else:
                     nc.scalar.copy(out=dst, in_=src)
-            return grouped
+            x_grouped[b] = grouped
 
-        def quantise_block(b, grouped):
+        def quantise_block(b):
             groups = slice(b * BLOCK, (b + 1) * BLOCK)
             nc.vector.quantize_mx(
                 out=x_codes[:, groups, :].rearrange("p g r -> p (g r)").bitcast(FP8X4),
                 scales=x_planes[:, groups, :].rearrange("p g r -> p (g r)"),
-                in_=grouped[:].rearrange("p g r t -> p (g r t)"),
+                in_=x_grouped[b][:].rearrange("p g r t -> p (g r t)"),
             )
+
+        acc = {}
+        for half in range(HALVES):
+            for e in range(ROW_TILES):
+                acc[(e, half)] = acc_pool.tile(
+                    [P, N_TILE], F32, name="acc_%d%d" % (e, half), tag="bank_%d" % (ROW_TILES * half + e)
+                )
+
+        def multiply_block(b):
+            for i in range(BLOCK):
+                g = b * BLOCK + i
+                for half in range(HALVES):
+                    cols = slice(half * N_TILE, (half + 1) * N_TILE)
+                    for e in range(ROW_TILES):
+                        rows = slice(e * P, (e + 1) * P)
+                        nc.tensor.matmul_mx(
+                            out=acc[(e, half)][:],
+                            lhsT=x_codes[:, g, rows].bitcast(FP8X4),
+                            lhsT_scale=x_planes[:, g, rows],
+                            rhs=w1_tiles[g][:, cols].bitcast(FP8X4),
+                            rhs_scale=w1_planes[PACK * i : P, b, cols],
+                            start=(g == 0),
+                            stop=(g == GROUPS1 - 1),
+                        )
 
         b1_sorted = keep.tile([P, GROUPS2, PACK, P], F32)
         b2_rows = keep.tile([P, H1], F32)
@@ -146,18 +170,18 @@ def tile_lintrans_pa_k_kernel(
 
         def spread_biases():
             for g2 in range(GROUPS2):
-                b1_ps = acc_pool.tile([P, K_PASS], F32, name="b1_ps", tag="bank_%d" % g2)
+                b1_ps = work_pool.tile([P, K_PASS], F32, name="b1_ps", tag="work")
                 nc.tensor.matmul(
                     b1_ps[:], lhsT=ones_bf[:], rhs=bias_rows[:, g2 * K_PASS : (g2 + 1) * K_PASS], start=True, stop=True
                 )
                 nc.vector.tensor_copy(out=b1_sorted[:, g2, :, :], in_=b1_ps[:].rearrange("r (p t) -> r t p", t=PACK))
-            b2_ps = acc_pool.tile([P, H1], F32, name="b2_ps", tag="bank_2")
+            b2_ps = work_pool.tile([P, H1], F32, name="b2_ps", tag="work")
             nc.tensor.matmul(b2_ps[:], lhsT=ones_bf[:], rhs=bias_rows[:, H0 : H0 + H1], start=True, stop=True)
             nc.vector.tensor_copy(out=b2_rows[:], in_=b2_ps[:])
             nc.vector.tensor_tensor(out=cl_shift[:], in0=cl_bf[:], in1=b2_rows[:], op=ALU.subtract)
 
         def transpose_centroids():
-            clT_ps = acc_pool.tile([P, J_TILES, P], F32, name="clT_ps", tag="bank_3")
+            clT_ps = work_pool.tile([P, J_TILES, P], F32, name="clT_ps", tag="work")
             for jt in range(J_TILES):
                 nc.tensor.transpose(clT_ps[:, jt, :], cl_shift[:, jt * P : (jt + 1) * P], ident[:])
             nc.vector.tensor_scalar_mul(out=c_m2[:], in0=clT_ps[:, :, 0:CENTROIDS], scalar1=-2.0)
@@ -166,7 +190,7 @@ def tile_lintrans_pa_k_kernel(
             )
 
         def centroid_norms():
-            cc_ps = acc_pool.tile([P, CENTROIDS], F32, name="cc_ps", tag="bank_0")
+            cc_ps = work_pool.tile([P, CENTROIDS], F32, name="cc_ps", tag="work")
             for jt in range(J_TILES):
                 nc.tensor.matmul(
                     cc_ps[:], lhsT=ones_f32[:], rhs=c_sq[:, jt, :], start=(jt == 0), stop=(jt == J_TILES - 1)
@@ -175,38 +199,31 @@ def tile_lintrans_pa_k_kernel(
 
         side_jobs = [spread_biases, transpose_centroids, centroid_norms]
 
-        waiting = transpose_block(0)
-        for b in range(1, BLOCKS):
-            fresh = transpose_block(b)
-            quantise_block(b - 1, waiting)
-            waiting = fresh
-            if b <= len(side_jobs):
-                side_jobs[b - 1]()
-        quantise_block(BLOCKS - 1, waiting)
-
-        acc = {}
-        for half in range(HALVES):
-            for e in range(ROW_TILES):
-                acc[(e, half)] = acc_pool.tile(
-                    [P, N_TILE], F32, name="acc_%d%d" % (e, half), tag="bank_%d" % (ROW_TILES * half + e)
-                )
-        for g in range(GROUPS1):
-            b, i = divmod(g, BLOCK)
-            for half in range(HALVES):
-                cols = slice(half * N_TILE, (half + 1) * N_TILE)
-                for e in range(ROW_TILES):
-                    rows = slice(e * P, (e + 1) * P)
-                    nc.tensor.matmul_mx(
-                        out=acc[(e, half)][:],
-                        lhsT=x_codes[:, g, rows].bitcast(FP8X4),
-                        lhsT_scale=x_planes[:, g, rows],
-                        rhs=w1_tiles[g][:, cols].bitcast(FP8X4),
-                        rhs_scale=w1_planes[PACK * i : P, b, cols],
-                        start=(g == 0),
-                        stop=(g == GROUPS1 - 1),
-                    )
-            if g + W1_BUFS < GROUPS1:
-                w1_tiles.append(load_w1(g + W1_BUFS))
+        for b in range(X_LEAD):
+            load_x(b)
+        load_w1(0)
+        load_x(X_LEAD)
+        load_w1(1)
+        w2_words = keep.tile([P, GROUPS2, H1], U32, align_bytes=64)
+        nc.sync.dma_start(
+            out=w2_words[:].bitcast(I32),
+            in_=W2_words.rearrange("g p n t -> p g (n t)").bitcast(I32),
+        )
+        for b in range(X_LEAD):
+            transpose_block(b)
+        quantise_block(0)
+        for b in range(BLOCKS):
+            if b + X_LEAD + 1 < BLOCKS:
+                load_x(b + X_LEAD + 1)
+            if b + 2 < BLOCKS:
+                load_w1(b + 2)
+            if b + 1 < BLOCKS:
+                quantise_block(b + 1)
+            multiply_block(b)
+            if b + X_LEAD < BLOCKS:
+                transpose_block(b + X_LEAD)
+            if b < len(side_jobs):
+                side_jobs[b]()
 
         h_grouped = keep.tile([P, GROUPS2, ROWS, PACK], BF16, align_bytes=64)
         h_codes = keep.tile([P, GROUPS2, ROWS], U32, align_bytes=64)

@@ -16,6 +16,12 @@ AXIS = mybir.AxisListType
 P = 128
 PACK = 4
 K_PASS = P * PACK
+QUADRANT = 32
+QUADRANTS = P // QUADRANT
+LIVE_ROWS = 4
+PSUM_BANKS = 8
+BANK_F32 = 512
+
 ROWS = 256
 ROW_TILES = ROWS // P
 D_IN = 16384
@@ -24,14 +30,15 @@ H1 = 256
 CENTROIDS = 20
 GROUPS1 = D_IN // K_PASS
 GROUPS2 = H0 // K_PASS
-N_TILE = 512
-HALVES = H0 // N_TILE
+HALVES = H0 // BANK_F32
 J_TILES = H1 // P
+WORDS = K_PASS // 2
+
 BLOCK = 4
 BLOCKS = GROUPS1 // BLOCK
-WORDS = K_PASS // 2
+SUM_BANKS = ROW_TILES * HALVES
+WORK_BANKS = PSUM_BANKS - SUM_BANKS
 W1_BUFS = 14
-X_LEAD = 2
 
 FLOPS = 2 * ROWS * D_IN * H0 + 2 * ROWS * H0 * H1 + 3 * ROWS * CENTROIDS * H1
 
@@ -43,13 +50,12 @@ def tile_lintrans_pa_k_kernel(
     with ExitStack() as stack:
         stack.enter_context(tc.manual_schedule())
         keep = stack.enter_context(tc.tile_pool(name="keep", bufs=1))
-        x_pool = stack.enter_context(tc.tile_pool(name="x_pool", bufs=X_LEAD + 1))
-        sorted_pool = stack.enter_context(tc.tile_pool(name="sorted_pool", bufs=2))
-        grouped_pool = stack.enter_context(tc.tile_pool(name="grouped_pool", bufs=2))
+        x_pool = stack.enter_context(tc.tile_pool(name="x_pool", bufs=BLOCKS))
+        grouped_pool = stack.enter_context(tc.tile_pool(name="grouped_pool", bufs=3))
         w1_pool = stack.enter_context(tc.tile_pool(name="w1_pool", bufs=W1_BUFS))
-        pre_pool = stack.enter_context(tc.tile_pool(name="pre_pool", bufs=4))
-        acc_pool = stack.enter_context(tc.psum_pool(name="acc_pool", bufs=1))
-        work_pool = stack.enter_context(tc.psum_pool(name="work_pool", bufs=4))
+        pre_pool = stack.enter_context(tc.tile_pool(name="pre_pool", bufs=SUM_BANKS))
+        sum_pool = stack.enter_context(tc.psum_pool(name="sum_pool", bufs=1))
+        work_pool = stack.enter_context(tc.psum_pool(name="work_pool", bufs=WORK_BANKS))
 
         bias_rows = keep.tile([P, H0 + H1], BF16)
         nc.vector.memset(bias_rows[:], 0.0)
@@ -57,12 +63,12 @@ def tile_lintrans_pa_k_kernel(
         nc.vector.memset(cl_bf[:], 0.0)
         silu_in = keep.tile([P, 1], F32)
         nc.vector.memset(silu_in[:], 0.0)
-        w1_planes = keep.tile([P, BLOCKS, H0], U8, align_bytes=64)
-        nc.vector.memset(w1_planes[:].bitcast(I32), 0)
-        w2_planes = keep.tile([P, GROUPS2, H1], U8, align_bytes=64)
-        nc.vector.memset(w2_planes[:].bitcast(I32), 0)
         ones_bf = keep.tile([P, P], BF16)
         nc.vector.memset(ones_bf[:], 1.0)
+        w1_scale_tiles = keep.tile([P, BLOCKS, H0], U8, align_bytes=64)
+        nc.vector.memset(w1_scale_tiles[:].bitcast(I32), 0)
+        w2_scale_tile = keep.tile([P, GROUPS2, H1], U8, align_bytes=64)
+        nc.vector.memset(w2_scale_tile[:].bitcast(I32), 0)
         ones_f32 = keep.tile([P, P], F32)
         nc.vector.memset(ones_f32[:], 1.0)
         ident = keep.tile([P, P], F32)
@@ -75,91 +81,70 @@ def tile_lintrans_pa_k_kernel(
         nc.scalar.activation(out=silu_out[:], in_=silu_in[:], func=ACT.Silu)
 
         for b in range(BLOCKS):
-            for quad in range(4):
+            for quad in range(QUADRANTS):
+                first = QUADRANT * quad
                 nc.gpsimd.dma_start(
-                    out=w1_planes[32 * quad : 32 * quad + 16, b, :].bitcast(F32),
-                    in_=W1_scales[b * BLOCK : (b + 1) * BLOCK, 4 * quad : 4 * quad + 4, :].bitcast(F32),
+                    out=w1_scale_tiles[first : first + BLOCK * LIVE_ROWS, b, :].bitcast(F32),
+                    in_=W1_scales[
+                        b * BLOCK : (b + 1) * BLOCK, LIVE_ROWS * quad : LIVE_ROWS * (quad + 1), :
+                    ].bitcast(F32),
                 )
-        for quad in range(4):
+        for quad in range(QUADRANTS):
+            first = QUADRANT * quad
             nc.gpsimd.dma_start(
-                out=w2_planes[32 * quad : 32 * quad + 4, :, :].bitcast(F32),
-                in_=W2_scales[:, 4 * quad : 4 * quad + 4, :].rearrange("g r n -> r g n").bitcast(F32),
+                out=w2_scale_tile[first : first + LIVE_ROWS, :, :].bitcast(F32),
+                in_=W2_scales[:, LIVE_ROWS * quad : LIVE_ROWS * (quad + 1), :]
+                .rearrange("g r n -> r g n")
+                .bitcast(F32),
             )
 
         x_view = x.rearrange("(p e) k -> p e k", e=ROW_TILES)
-        w1_view = W1_words.rearrange("g p n t -> g p (n t)").bitcast(I32)
-        x_codes = keep.tile([P, GROUPS1, ROWS], U32, align_bytes=64)
-        x_planes = keep.tile([P, GROUPS1, ROWS], U8, align_bytes=64)
-        x_raw = {}
-        x_grouped = {}
-        w1_tiles = {}
-
-        def load_x(b):
+        x_blocks = []
+        for b in range(BLOCKS):
             x_block = x_pool.tile([P, ROW_TILES, BLOCK * K_PASS], BF16, name="x_block")
             k_cols = slice(b * BLOCK * K_PASS, (b + 1) * BLOCK * K_PASS)
             nc.sync.dma_start(out=x_block[:], in_=x_view[:, :, k_cols])
-            x_raw[b] = x_block
+            x_blocks.append(x_block)
 
-        def load_w1(b):
-            for g in range(b * BLOCK, (b + 1) * BLOCK):
-                w1_group = w1_pool.tile([P, H0], U32, name="w1_group", align_bytes=64)
-                nc.sync.dma_start(out=w1_group[:].bitcast(I32), in_=w1_view[g])
-                w1_tiles[g] = w1_group
+        w1_view = W1_words.rearrange("g p n t -> g p (n t)").bitcast(I32)
+
+        def load_w1(g):
+            w1_group = w1_pool.tile([P, H0], U32, name="w1_group", align_bytes=64)
+            nc.sync.dma_start(out=w1_group[:].bitcast(I32), in_=w1_view[g])
+            return w1_group
+
+        w1_groups = [load_w1(g) for g in range(W1_BUFS)]
+
+        x_codes = keep.tile([P, GROUPS1, ROWS], U32, align_bytes=64)
+        x_scales = keep.tile([P, GROUPS1, ROWS], U8, align_bytes=64)
 
         def transpose_block(b):
-            x_sorted = sorted_pool.tile([P, ROW_TILES, BLOCK, 2, P], F32, name="x_sorted")
-            x_words = x_raw[b][:].bitcast(F32)
-            nc.vector.tensor_copy(
-                out=x_sorted[:, 0, :, :, :], in_=x_words[:, 0, :].rearrange("r (i p u) -> r i u p", i=BLOCK, u=2)
-            )
-            nc.scalar.copy(
-                out=x_sorted[:, 1, :, :, :], in_=x_words[:, 1, :].rearrange("r (i p u) -> r i u p", i=BLOCK, u=2)
-            )
             grouped = grouped_pool.tile([P, BLOCK, ROWS, PACK], BF16, name="grouped", align_bytes=64)
+            x_words = x_blocks[b][:].bitcast(F32)
             for i in range(BLOCK):
-                xt = work_pool.tile([P, 2, ROWS], F32, name="xt", tag="work")
+                turned = work_pool.tile([P, 2, ROWS], F32, name="turned", tag="work")
                 for u in range(2):
                     for e in range(ROW_TILES):
-                        nc.tensor.transpose(xt[:, u, e * P : (e + 1) * P], x_sorted[:, e, i, u, :], ident[:])
-                dst = grouped[:, i, :, :].bitcast(F32)
-                src = xt[:].rearrange("p u r -> p r u")
+                        nc.tensor.transpose(
+                            turned[:, u, e * P : (e + 1) * P],
+                            x_words[:, e, WORDS * i + u : WORDS * (i + 1) : 2],
+                            ident[:],
+                        )
+                side_by_side = grouped[:, i, :, :].bitcast(F32)
+                alternately = turned[:].rearrange("p u r -> p r u")
                 if i == BLOCK - 1:
-                    nc.vector.tensor_copy(out=dst, in_=src)
+                    nc.vector.tensor_copy(out=side_by_side, in_=alternately)
                 else:
-                    nc.scalar.copy(out=dst, in_=src)
-            x_grouped[b] = grouped
+                    nc.scalar.copy(out=side_by_side, in_=alternately)
+            return grouped
 
-        def quantise_block(b):
+        def quantise_block(b, grouped):
             groups = slice(b * BLOCK, (b + 1) * BLOCK)
             nc.vector.quantize_mx(
                 out=x_codes[:, groups, :].rearrange("p g r -> p (g r)").bitcast(FP8X4),
-                scales=x_planes[:, groups, :].rearrange("p g r -> p (g r)"),
-                in_=x_grouped[b][:].rearrange("p g r t -> p (g r t)"),
+                scales=x_scales[:, groups, :].rearrange("p g r -> p (g r)"),
+                in_=grouped[:].rearrange("p g r t -> p (g r t)"),
             )
-
-        acc = {}
-        for half in range(HALVES):
-            for e in range(ROW_TILES):
-                acc[(e, half)] = acc_pool.tile(
-                    [P, N_TILE], F32, name="acc_%d%d" % (e, half), tag="bank_%d" % (ROW_TILES * half + e)
-                )
-
-        def multiply_block(b):
-            for i in range(BLOCK):
-                g = b * BLOCK + i
-                for half in range(HALVES):
-                    cols = slice(half * N_TILE, (half + 1) * N_TILE)
-                    for e in range(ROW_TILES):
-                        rows = slice(e * P, (e + 1) * P)
-                        nc.tensor.matmul_mx(
-                            out=acc[(e, half)][:],
-                            lhsT=x_codes[:, g, rows].bitcast(FP8X4),
-                            lhsT_scale=x_planes[:, g, rows],
-                            rhs=w1_tiles[g][:, cols].bitcast(FP8X4),
-                            rhs_scale=w1_planes[PACK * i : P, b, cols],
-                            start=(g == 0),
-                            stop=(g == GROUPS1 - 1),
-                        )
 
         b1_sorted = keep.tile([P, GROUPS2, PACK, P], F32)
         b2_rows = keep.tile([P, H1], F32)
@@ -170,18 +155,18 @@ def tile_lintrans_pa_k_kernel(
 
         def spread_biases():
             for g2 in range(GROUPS2):
-                b1_ps = work_pool.tile([P, K_PASS], F32, name="b1_ps", tag="work")
+                b1_ps = sum_pool.tile([P, K_PASS], F32, name="b1_ps", tag="sum_%d" % g2)
                 nc.tensor.matmul(
                     b1_ps[:], lhsT=ones_bf[:], rhs=bias_rows[:, g2 * K_PASS : (g2 + 1) * K_PASS], start=True, stop=True
                 )
                 nc.vector.tensor_copy(out=b1_sorted[:, g2, :, :], in_=b1_ps[:].rearrange("r (p t) -> r t p", t=PACK))
-            b2_ps = work_pool.tile([P, H1], F32, name="b2_ps", tag="work")
+            b2_ps = sum_pool.tile([P, H1], F32, name="b2_ps", tag="sum_2")
             nc.tensor.matmul(b2_ps[:], lhsT=ones_bf[:], rhs=bias_rows[:, H0 : H0 + H1], start=True, stop=True)
             nc.vector.tensor_copy(out=b2_rows[:], in_=b2_ps[:])
             nc.vector.tensor_tensor(out=cl_shift[:], in0=cl_bf[:], in1=b2_rows[:], op=ALU.subtract)
 
         def transpose_centroids():
-            clT_ps = work_pool.tile([P, J_TILES, P], F32, name="clT_ps", tag="work")
+            clT_ps = sum_pool.tile([P, J_TILES, P], F32, name="clT_ps", tag="sum_3")
             for jt in range(J_TILES):
                 nc.tensor.transpose(clT_ps[:, jt, :], cl_shift[:, jt * P : (jt + 1) * P], ident[:])
             nc.vector.tensor_scalar_mul(out=c_m2[:], in0=clT_ps[:, :, 0:CENTROIDS], scalar1=-2.0)
@@ -190,7 +175,7 @@ def tile_lintrans_pa_k_kernel(
             )
 
         def centroid_norms():
-            cc_ps = work_pool.tile([P, CENTROIDS], F32, name="cc_ps", tag="work")
+            cc_ps = sum_pool.tile([P, CENTROIDS], F32, name="cc_ps", tag="sum_0")
             for jt in range(J_TILES):
                 nc.tensor.matmul(
                     cc_ps[:], lhsT=ones_f32[:], rhs=c_sq[:, jt, :], start=(jt == 0), stop=(jt == J_TILES - 1)
@@ -199,103 +184,116 @@ def tile_lintrans_pa_k_kernel(
 
         side_jobs = [spread_biases, transpose_centroids, centroid_norms]
 
-        for b in range(X_LEAD):
-            load_x(b)
-        load_w1(0)
-        load_x(X_LEAD)
-        load_w1(1)
+        waiting = None
+        for b in range(BLOCKS):
+            if b < len(side_jobs):
+                side_jobs[b]()
+            fresh = transpose_block(b)
+            if b > 0:
+                quantise_block(b - 1, waiting)
+            waiting = fresh
+        quantise_block(BLOCKS - 1, waiting)
+
+        sums = {}
+        for half in range(HALVES):
+            for e in range(ROW_TILES):
+                sums[(e, half)] = sum_pool.tile(
+                    [P, BANK_F32], F32, name="sums_%d%d" % (e, half), tag="sum_%d" % (ROW_TILES * half + e)
+                )
+        for g in range(GROUPS1):
+            b, i = divmod(g, BLOCK)
+            for half in range(HALVES):
+                cols = slice(half * BANK_F32, (half + 1) * BANK_F32)
+                for e in range(ROW_TILES):
+                    rows = slice(e * P, (e + 1) * P)
+                    nc.tensor.matmul_mx(
+                        out=sums[(e, half)][:],
+                        lhsT=x_codes[:, g, rows].bitcast(FP8X4),
+                        lhsT_scale=x_scales[:, g, rows],
+                        rhs=w1_groups[g][:, cols].bitcast(FP8X4),
+                        rhs_scale=w1_scale_tiles[LIVE_ROWS * i : P, b, cols],
+                        start=(g == 0),
+                        stop=(g == GROUPS1 - 1),
+                    )
+            if g + W1_BUFS < GROUPS1:
+                w1_groups.append(load_w1(g + W1_BUFS))
         w2_words = keep.tile([P, GROUPS2, H1], U32, align_bytes=64)
         nc.sync.dma_start(
             out=w2_words[:].bitcast(I32),
             in_=W2_words.rearrange("g p n t -> p g (n t)").bitcast(I32),
         )
-        for b in range(X_LEAD):
-            transpose_block(b)
-        quantise_block(0)
-        for b in range(BLOCKS):
-            if b + X_LEAD + 1 < BLOCKS:
-                load_x(b + X_LEAD + 1)
-            if b + 2 < BLOCKS:
-                load_w1(b + 2)
-            if b + 1 < BLOCKS:
-                quantise_block(b + 1)
-            multiply_block(b)
-            if b + X_LEAD < BLOCKS:
-                transpose_block(b + X_LEAD)
-            if b < len(side_jobs):
-                side_jobs[b]()
 
         h_grouped = keep.tile([P, GROUPS2, ROWS, PACK], BF16, align_bytes=64)
         h_codes = keep.tile([P, GROUPS2, ROWS], U32, align_bytes=64)
-        h_planes = keep.tile([P, GROUPS2, ROWS], U8, align_bytes=64)
+        h_scales = keep.tile([P, GROUPS2, ROWS], U8, align_bytes=64)
         for g2 in range(GROUPS2):
             for e in range(ROW_TILES):
                 pre = pre_pool.tile([P, PACK, P], F32, name="pre")
                 nc.vector.tensor_tensor(
                     out=pre[:],
-                    in0=acc[(e, g2)][:].rearrange("r (p t) -> r t p", t=PACK),
+                    in0=sums[(e, g2)][:].rearrange("r (p t) -> r t p", t=PACK),
                     in1=b1_sorted[:, g2, :, :],
                     op=ALU.add,
                 )
-                preT = work_pool.tile([P, PACK, P], F32, name="preT", tag="work")
+                pre_turned = work_pool.tile([P, PACK, P], F32, name="pre_turned", tag="work")
                 for t in range(PACK):
-                    nc.tensor.transpose(preT[:, t, :], pre[:, t, :], ident[:])
+                    nc.tensor.transpose(pre_turned[:, t, :], pre[:, t, :], ident[:])
                 nc.scalar.activation(
                     out=h_grouped[:, g2, e * P : (e + 1) * P, :],
-                    in_=preT[:].rearrange("p t r -> p r t"),
+                    in_=pre_turned[:].rearrange("p t r -> p r t"),
                     func=ACT.Silu,
                 )
         for g2 in range(GROUPS2):
             nc.vector.quantize_mx(
                 out=h_codes[:, g2, :].bitcast(FP8X4),
-                scales=h_planes[:, g2, :],
+                scales=h_scales[:, g2, :],
                 in_=h_grouped[:, g2, :, :].rearrange("p r t -> p (r t)"),
             )
 
-        zT_ps = [acc_pool.tile([P, ROWS], F32, name="zT_ps%d" % jt, tag="bank_%d" % jt) for jt in range(J_TILES)]
-        z_ps = [acc_pool.tile([P, H1], F32, name="z_ps%d" % e, tag="bank_%d" % (J_TILES + e)) for e in range(ROW_TILES)]
+        aT_ps = [sum_pool.tile([P, ROWS], F32, name="aT_ps%d" % jt, tag="sum_%d" % jt) for jt in range(J_TILES)]
+        a_ps = [sum_pool.tile([P, H1], F32, name="a_ps%d" % e, tag="sum_%d" % (J_TILES + e)) for e in range(ROW_TILES)]
         for g2 in range(GROUPS2):
             for jt in range(J_TILES):
                 j_cols = slice(jt * P, (jt + 1) * P)
                 nc.tensor.matmul_mx(
-                    out=zT_ps[jt][:],
+                    out=aT_ps[jt][:],
                     lhsT=w2_words[:, g2, j_cols].bitcast(FP8X4),
-                    lhsT_scale=w2_planes[:, g2, j_cols],
+                    lhsT_scale=w2_scale_tile[:, g2, j_cols],
                     rhs=h_codes[:, g2, :].bitcast(FP8X4),
-                    rhs_scale=h_planes[:, g2, :],
+                    rhs_scale=h_scales[:, g2, :],
                     start=(g2 == 0),
                     stop=(g2 == GROUPS2 - 1),
                 )
             for e in range(ROW_TILES):
                 rows = slice(e * P, (e + 1) * P)
                 nc.tensor.matmul_mx(
-                    out=z_ps[e][:],
+                    out=a_ps[e][:],
                     lhsT=h_codes[:, g2, rows].bitcast(FP8X4),
-                    lhsT_scale=h_planes[:, g2, rows],
+                    lhsT_scale=h_scales[:, g2, rows],
                     rhs=w2_words[:, g2, :].bitcast(FP8X4),
-                    rhs_scale=w2_planes[:, g2, :],
+                    rhs_scale=w2_scale_tile[:, g2, :],
                     start=(g2 == 0),
                     stop=(g2 == GROUPS2 - 1),
                 )
 
-        zT = keep.tile([P, J_TILES, ROWS], F32)
-        nc.scalar.copy(out=zT[:, 0, :], in_=zT_ps[0][:])
-        nc.vector.tensor_copy(out=zT[:, 1, :], in_=zT_ps[1][:])
-        z_sq = keep.tile([P, ROW_TILES, H1], F32)
-        zz = keep.tile([P, ROW_TILES], F32)
+        aT = keep.tile([P, J_TILES, ROWS], F32)
+        nc.scalar.copy(out=aT[:, 0, :], in_=aT_ps[0][:])
+        nc.vector.tensor_copy(out=aT[:, 1, :], in_=aT_ps[1][:])
+        a_sq = keep.tile([P, ROW_TILES, H1], F32)
+        aa = keep.tile([P, ROW_TILES], F32)
         for e in range(ROW_TILES):
-            nc.scalar.activation(out=z_sq[:, e, :], in_=z_ps[e][:], func=ACT.Square, accum_out=zz[:, e : e + 1])
+            nc.scalar.activation(out=a_sq[:, e, :], in_=a_ps[e][:], func=ACT.Square, accum_out=aa[:, e : e + 1])
         z = keep.tile([P, ROW_TILES, H1], F32)
         for e in range(ROW_TILES):
-            nc.vector.tensor_tensor(out=z[:, e, :], in0=z_ps[e][:], in1=b2_rows[:], op=ALU.add)
+            nc.vector.tensor_tensor(out=z[:, e, :], in0=a_ps[e][:], in1=b2_rows[:], op=ALU.add)
         nc.sync.dma_start(out=out_0.rearrange("(p e) j -> p e j", e=ROW_TILES), in_=z[:])
 
-        dots = work_pool.tile([P, ROW_TILES, 32], F32, name="dots", tag="work")
+        dots = work_pool.tile([P, ROW_TILES, CENTROIDS], F32, name="dots", tag="work")
         for e in range(ROW_TILES):
             for jt in range(J_TILES):
                 nc.tensor.matmul(
-                    dots[:, e, 0:CENTROIDS],
-                    lhsT=zT[:, jt, e * P : (e + 1) * P],
+                    dots[:, e, :],
+                    lhsT=aT[:, jt, e * P : (e + 1) * P],
                     rhs=c_m2[:, jt, :],
                     start=(jt == 0),
                     stop=(jt == J_TILES - 1),
@@ -304,8 +302,8 @@ def tile_lintrans_pa_k_kernel(
         for e in range(ROW_TILES):
             nc.vector.scalar_tensor_tensor(
                 out=one_plus_d2[:, e, :],
-                in0=dots[:, e, 0:CENTROIDS],
-                scalar=zz[:, e : e + 1],
+                in0=dots[:, e, :],
+                scalar=aa[:, e : e + 1],
                 in1=cc1[:],
                 op0=ALU.add,
                 op1=ALU.add,

@@ -38,6 +38,8 @@ BLOCK = 4
 BLOCKS = GROUPS1 // BLOCK
 SUM_BANKS = ROW_TILES * HALVES
 WORK_BANKS = PSUM_BANKS - SUM_BANKS
+X_AHEAD = 3
+RUN = 2
 W1_BUFS = 14
 
 FLOPS = 2 * ROWS * D_IN * H0 + 2 * ROWS * H0 * H1 + 3 * ROWS * CENTROIDS * H1
@@ -100,7 +102,8 @@ def tile_lintrans_pa_k_kernel(
 
         x_view = x.rearrange("(p e) k -> p e k", e=ROW_TILES)
         x_blocks = []
-        for b in range(BLOCKS):
+
+        def load_x(b):
             x_block = x_pool.tile([P, ROW_TILES, BLOCK * K_PASS], BF16, name="x_block")
             k_cols = slice(b * BLOCK * K_PASS, (b + 1) * BLOCK * K_PASS)
             nc.sync.dma_start(out=x_block[:], in_=x_view[:, :, k_cols])
@@ -113,12 +116,18 @@ def tile_lintrans_pa_k_kernel(
             nc.sync.dma_start(out=w1_group[:].bitcast(I32), in_=w1_view[g])
             return w1_group
 
-        w1_groups = [load_w1(g) for g in range(W1_BUFS)]
+        w1_groups = []
+        for b in range(BLOCKS):
+            load_x(b)
+            if b >= X_AHEAD:
+                w1_groups.append(load_w1(b - X_AHEAD))
+        for g in range(BLOCKS - X_AHEAD, W1_BUFS):
+            w1_groups.append(load_w1(g))
 
         x_codes = keep.tile([P, GROUPS1, ROWS], U32, align_bytes=64)
         x_scales = keep.tile([P, GROUPS1, ROWS], U8, align_bytes=64)
 
-        def transpose_block(b):
+        def transpose_block(b, after_run):
             grouped = grouped_pool.tile([P, BLOCK, ROWS, PACK], BF16, name="grouped", align_bytes=64)
             x_words = x_blocks[b][:].bitcast(F32)
             for i in range(BLOCK):
@@ -136,6 +145,8 @@ def tile_lintrans_pa_k_kernel(
                     nc.vector.tensor_copy(out=side_by_side, in_=alternately)
                 else:
                     nc.scalar.copy(out=side_by_side, in_=alternately)
+                if (i + 1) % RUN == 0:
+                    after_run(i // RUN)
             return grouped
 
         def quantise_block(b, grouped):
@@ -184,39 +195,49 @@ def tile_lintrans_pa_k_kernel(
 
         side_jobs = [spread_biases, transpose_centroids, centroid_norms]
 
+        sums = {}
+
+        def open_sums():
+            for half in range(HALVES):
+                for e in range(ROW_TILES):
+                    sums[(e, half)] = sum_pool.tile(
+                        [P, BANK_F32], F32, name="sums_%d%d" % (e, half), tag="sum_%d" % (ROW_TILES * half + e)
+                    )
+
+        def passes(g, half):
+            b, i = divmod(g, BLOCK)
+            cols = slice(half * BANK_F32, (half + 1) * BANK_F32)
+            for e in range(ROW_TILES):
+                rows = slice(e * P, (e + 1) * P)
+                nc.tensor.matmul_mx(
+                    out=sums[(e, half)][:],
+                    lhsT=x_codes[:, g, rows].bitcast(FP8X4),
+                    lhsT_scale=x_scales[:, g, rows],
+                    rhs=w1_groups[g][:, cols].bitcast(FP8X4),
+                    rhs_scale=w1_scale_tiles[LIVE_ROWS * i : P, b, cols],
+                    start=(g == 0),
+                    stop=(g == GROUPS1 - 1),
+                )
+            if half == HALVES - 1 and g + W1_BUFS < GROUPS1:
+                w1_groups.append(load_w1(g + W1_BUFS))
+
         waiting = None
         for b in range(BLOCKS):
             if b < len(side_jobs):
                 side_jobs[b]()
-            fresh = transpose_block(b)
+            if b == X_AHEAD:
+                open_sums()
+            if b >= X_AHEAD:
+                fresh = transpose_block(b, lambda half, g=b - X_AHEAD: passes(g, half))
+            else:
+                fresh = transpose_block(b, lambda half: None)
             if b > 0:
                 quantise_block(b - 1, waiting)
             waiting = fresh
         quantise_block(BLOCKS - 1, waiting)
-
-        sums = {}
-        for half in range(HALVES):
-            for e in range(ROW_TILES):
-                sums[(e, half)] = sum_pool.tile(
-                    [P, BANK_F32], F32, name="sums_%d%d" % (e, half), tag="sum_%d" % (ROW_TILES * half + e)
-                )
-        for g in range(GROUPS1):
-            b, i = divmod(g, BLOCK)
+        for g in range(BLOCKS - X_AHEAD, GROUPS1):
             for half in range(HALVES):
-                cols = slice(half * BANK_F32, (half + 1) * BANK_F32)
-                for e in range(ROW_TILES):
-                    rows = slice(e * P, (e + 1) * P)
-                    nc.tensor.matmul_mx(
-                        out=sums[(e, half)][:],
-                        lhsT=x_codes[:, g, rows].bitcast(FP8X4),
-                        lhsT_scale=x_scales[:, g, rows],
-                        rhs=w1_groups[g][:, cols].bitcast(FP8X4),
-                        rhs_scale=w1_scale_tiles[LIVE_ROWS * i : P, b, cols],
-                        start=(g == 0),
-                        stop=(g == GROUPS1 - 1),
-                    )
-            if g + W1_BUFS < GROUPS1:
-                w1_groups.append(load_w1(g + W1_BUFS))
+                passes(g, half)
         w2_words = keep.tile([P, GROUPS2, H1], U32, align_bytes=64)
         nc.sync.dma_start(
             out=w2_words[:].bitcast(I32),

from contextlib import ExitStack

import concourse.mybir as mybir
from concourse.masks import make_identity

F32 = mybir.dt.float32
BF16 = mybir.dt.bfloat16
I32 = mybir.dt.int32
U32 = mybir.dt.uint32
U8 = mybir.dt.uint8
FP8X4 = mybir.dt.float8_e4m3fn_x4
ACT = mybir.ActivationFunctionType
ALU = mybir.AluOpType
AXIS = mybir.AxisListType

P = 128
PACK = 4
K_PASS = P * PACK
QUADRANT = 32
QUADRANTS = P // QUADRANT
LIVE_ROWS = 4
PSUM_BANKS = 8
BANK_F32 = 512

ROWS = 256
ROW_TILES = ROWS // P
D_IN = 16384
H0 = 1024
H1 = 256
CENTROIDS = 20
GROUPS1 = D_IN // K_PASS
GROUPS2 = H0 // K_PASS
HALVES = H0 // BANK_F32
J_TILES = H1 // P
WORDS = K_PASS // 2

BLOCK = 4
BLOCKS = GROUPS1 // BLOCK
SUM_BANKS = ROW_TILES * HALVES
WORK_BANKS = PSUM_BANKS - SUM_BANKS
X_AHEAD = 3
RUN = 2
W1_BUFS = 14

FLOPS = 2 * ROWS * D_IN * H0 + 2 * ROWS * H0 * H1 + 3 * ROWS * CENTROIDS * H1


def tile_lintrans_pa_k_kernel(
    tc, x, W1_words, W1_scales, b1, W2_words, W2_scales, b2, clusters, out_0, out_1
):
    nc = tc.nc
    with ExitStack() as stack:
        stack.enter_context(tc.manual_schedule())
        keep = stack.enter_context(tc.tile_pool(name="keep", bufs=1))
        x_pool = stack.enter_context(tc.tile_pool(name="x_pool", bufs=BLOCKS))
        grouped_pool = stack.enter_context(tc.tile_pool(name="grouped_pool", bufs=3))
        w1_pool = stack.enter_context(tc.tile_pool(name="w1_pool", bufs=W1_BUFS))
        pre_pool = stack.enter_context(tc.tile_pool(name="pre_pool", bufs=SUM_BANKS))
        sum_pool = stack.enter_context(tc.psum_pool(name="sum_pool", bufs=1))
        work_pool = stack.enter_context(tc.psum_pool(name="work_pool", bufs=WORK_BANKS))

        bias_rows = keep.tile([P, H0 + H1], BF16)
        nc.vector.memset(bias_rows[:], 0.0)
        cl_bf = keep.tile([P, H1], BF16)
        nc.vector.memset(cl_bf[:], 0.0)
        silu_in = keep.tile([P, 1], F32)
        nc.vector.memset(silu_in[:], 0.0)
        ones_bf = keep.tile([P, P], BF16)
        nc.vector.memset(ones_bf[:], 1.0)
        w1_scale_tiles = keep.tile([P, BLOCKS, H0], U8, align_bytes=64)
        nc.vector.memset(w1_scale_tiles[:].bitcast(I32), 0)
        w2_scale_tile = keep.tile([P, GROUPS2, H1], U8, align_bytes=64)
        nc.vector.memset(w2_scale_tile[:].bitcast(I32), 0)
        ones_f32 = keep.tile([P, P], F32)
        nc.vector.memset(ones_f32[:], 1.0)
        ident = keep.tile([P, P], F32)
        make_identity(nc, ident[:])

        nc.scalar.dma_start(out=bias_rows[0:1, 0:H0], in_=b1.unsqueeze(0))
        nc.scalar.dma_start(out=bias_rows[0:1, H0 : H0 + H1], in_=b2.unsqueeze(0))
        nc.scalar.dma_start(out=cl_bf[0:CENTROIDS, :], in_=clusters)
        silu_out = keep.tile([P, 1], F32)
        nc.scalar.activation(out=silu_out[:], in_=silu_in[:], func=ACT.Silu)

        for b in range(BLOCKS):
            for quad in range(QUADRANTS):
                first = QUADRANT * quad
                nc.gpsimd.dma_start(
                    out=w1_scale_tiles[first : first + BLOCK * LIVE_ROWS, b, :].bitcast(F32),
                    in_=W1_scales[
                        b * BLOCK : (b + 1) * BLOCK, LIVE_ROWS * quad : LIVE_ROWS * (quad + 1), :
                    ].bitcast(F32),
                )
        for quad in range(QUADRANTS):
            first = QUADRANT * quad
            nc.gpsimd.dma_start(
                out=w2_scale_tile[first : first + LIVE_ROWS, :, :].bitcast(F32),
                in_=W2_scales[:, LIVE_ROWS * quad : LIVE_ROWS * (quad + 1), :]
                .rearrange("g r n -> r g n")
                .bitcast(F32),
            )

        x_view = x.rearrange("(p e) k -> p e k", e=ROW_TILES)
        x_blocks = []

        def load_x(b):
            x_block = x_pool.tile([P, ROW_TILES, BLOCK * K_PASS], BF16, name="x_block")
            k_cols = slice(b * BLOCK * K_PASS, (b + 1) * BLOCK * K_PASS)
            nc.sync.dma_start(out=x_block[:], in_=x_view[:, :, k_cols])
            x_blocks.append(x_block)

        w1_view = W1_words.rearrange("g p n t -> g p (n t)").bitcast(I32)

        def load_w1(g):
            w1_group = w1_pool.tile([P, H0], U32, name="w1_group", align_bytes=64)
            nc.sync.dma_start(out=w1_group[:].bitcast(I32), in_=w1_view[g])
            return w1_group

        w1_groups = []
        for b in range(BLOCKS):
            load_x(b)
            if b >= X_AHEAD:
                w1_groups.append(load_w1(b - X_AHEAD))
        for g in range(BLOCKS - X_AHEAD, W1_BUFS):
            w1_groups.append(load_w1(g))

        x_codes = keep.tile([P, GROUPS1, ROWS], U32, align_bytes=64)
        x_scales = keep.tile([P, GROUPS1, ROWS], U8, align_bytes=64)

        def transpose_block(b, after_run):
            grouped = grouped_pool.tile([P, BLOCK, ROWS, PACK], BF16, name="grouped", align_bytes=64)
            x_words = x_blocks[b][:].bitcast(F32)
            for i in range(BLOCK):
                turned = work_pool.tile([P, 2, ROWS], F32, name="turned", tag="work")
                for u in range(2):
                    for e in range(ROW_TILES):
                        nc.tensor.transpose(
                            turned[:, u, e * P : (e + 1) * P],
                            x_words[:, e, WORDS * i + u : WORDS * (i + 1) : 2],
                            ident[:],
                        )
                side_by_side = grouped[:, i, :, :].bitcast(F32)
                alternately = turned[:].rearrange("p u r -> p r u")
                if i == BLOCK - 1:
                    nc.vector.tensor_copy(out=side_by_side, in_=alternately)
                else:
                    nc.scalar.copy(out=side_by_side, in_=alternately)
                if (i + 1) % RUN == 0:
                    after_run(i // RUN)
            return grouped

        def quantise_block(b, grouped):
            groups = slice(b * BLOCK, (b + 1) * BLOCK)
            nc.vector.quantize_mx(
                out=x_codes[:, groups, :].rearrange("p g r -> p (g r)").bitcast(FP8X4),
                scales=x_scales[:, groups, :].rearrange("p g r -> p (g r)"),
                in_=grouped[:].rearrange("p g r t -> p (g r t)"),
            )

        b1_sorted = keep.tile([P, GROUPS2, PACK, P], F32)
        b2_rows = keep.tile([P, H1], F32)
        cl_shift = keep.tile([P, H1], F32)
        c_m2 = keep.tile([P, J_TILES, CENTROIDS], F32)
        c_sq = keep.tile([P, J_TILES, CENTROIDS], F32)
        cc1 = keep.tile([P, CENTROIDS], F32)

        def spread_biases():
            for g2 in range(GROUPS2):
                b1_ps = sum_pool.tile([P, K_PASS], F32, name="b1_ps", tag="sum_%d" % g2)
                nc.tensor.matmul(
                    b1_ps[:], lhsT=ones_bf[:], rhs=bias_rows[:, g2 * K_PASS : (g2 + 1) * K_PASS], start=True, stop=True
                )
                nc.vector.tensor_copy(out=b1_sorted[:, g2, :, :], in_=b1_ps[:].rearrange("r (p t) -> r t p", t=PACK))
            b2_ps = sum_pool.tile([P, H1], F32, name="b2_ps", tag="sum_2")
            nc.tensor.matmul(b2_ps[:], lhsT=ones_bf[:], rhs=bias_rows[:, H0 : H0 + H1], start=True, stop=True)
            nc.vector.tensor_copy(out=b2_rows[:], in_=b2_ps[:])
            nc.vector.tensor_tensor(out=cl_shift[:], in0=cl_bf[:], in1=b2_rows[:], op=ALU.subtract)

        def transpose_centroids():
            clT_ps = sum_pool.tile([P, J_TILES, P], F32, name="clT_ps", tag="sum_3")
            for jt in range(J_TILES):
                nc.tensor.transpose(clT_ps[:, jt, :], cl_shift[:, jt * P : (jt + 1) * P], ident[:])
            nc.vector.tensor_scalar_mul(out=c_m2[:], in0=clT_ps[:, :, 0:CENTROIDS], scalar1=-2.0)
            nc.vector.scalar_tensor_tensor(
                out=c_sq[:], in0=c_m2[:], scalar=0.25, in1=c_m2[:], op0=ALU.mult, op1=ALU.mult
            )

        def centroid_norms():
            cc_ps = sum_pool.tile([P, CENTROIDS], F32, name="cc_ps", tag="sum_0")
            for jt in range(J_TILES):
                nc.tensor.matmul(
                    cc_ps[:], lhsT=ones_f32[:], rhs=c_sq[:, jt, :], start=(jt == 0), stop=(jt == J_TILES - 1)
                )
            nc.vector.tensor_scalar_add(out=cc1[:], in0=cc_ps[:], scalar1=1.0)

        side_jobs = [spread_biases, transpose_centroids, centroid_norms]

        sums = {}

        def open_sums():
            for half in range(HALVES):
                for e in range(ROW_TILES):
                    sums[(e, half)] = sum_pool.tile(
                        [P, BANK_F32], F32, name="sums_%d%d" % (e, half), tag="sum_%d" % (ROW_TILES * half + e)
                    )

        def passes(g, half):
            b, i = divmod(g, BLOCK)
            cols = slice(half * BANK_F32, (half + 1) * BANK_F32)
            for e in range(ROW_TILES):
                rows = slice(e * P, (e + 1) * P)
                nc.tensor.matmul_mx(
                    out=sums[(e, half)][:],
                    lhsT=x_codes[:, g, rows].bitcast(FP8X4),
                    lhsT_scale=x_scales[:, g, rows],
                    rhs=w1_groups[g][:, cols].bitcast(FP8X4),
                    rhs_scale=w1_scale_tiles[LIVE_ROWS * i : P, b, cols],
                    start=(g == 0),
                    stop=(g == GROUPS1 - 1),
                )
            if half == HALVES - 1 and g + W1_BUFS < GROUPS1:
                w1_groups.append(load_w1(g + W1_BUFS))

        waiting = None
        for b in range(BLOCKS):
            if b < len(side_jobs):
                side_jobs[b]()
            if b == X_AHEAD:
                open_sums()
            if b >= X_AHEAD:
                fresh = transpose_block(b, lambda half, g=b - X_AHEAD: passes(g, half))
            else:
                fresh = transpose_block(b, lambda half: None)
            if b > 0:
                quantise_block(b - 1, waiting)
            waiting = fresh
        quantise_block(BLOCKS - 1, waiting)
        for g in range(BLOCKS - X_AHEAD, GROUPS1):
            for half in range(HALVES):
                passes(g, half)
        w2_words = keep.tile([P, GROUPS2, H1], U32, align_bytes=64)
        nc.sync.dma_start(
            out=w2_words[:].bitcast(I32),
            in_=W2_words.rearrange("g p n t -> p g (n t)").bitcast(I32),
        )

        h_grouped = keep.tile([P, GROUPS2, ROWS, PACK], BF16, align_bytes=64)
        h_codes = keep.tile([P, GROUPS2, ROWS], U32, align_bytes=64)
        h_scales = keep.tile([P, GROUPS2, ROWS], U8, align_bytes=64)
        for g2 in range(GROUPS2):
            for e in range(ROW_TILES):
                pre = pre_pool.tile([P, PACK, P], F32, name="pre")
                nc.vector.tensor_tensor(
                    out=pre[:],
                    in0=sums[(e, g2)][:].rearrange("r (p t) -> r t p", t=PACK),
                    in1=b1_sorted[:, g2, :, :],
                    op=ALU.add,
                )
                pre_turned = work_pool.tile([P, PACK, P], F32, name="pre_turned", tag="work")
                for t in range(PACK):
                    nc.tensor.transpose(pre_turned[:, t, :], pre[:, t, :], ident[:])
                nc.scalar.activation(
                    out=h_grouped[:, g2, e * P : (e + 1) * P, :],
                    in_=pre_turned[:].rearrange("p t r -> p r t"),
                    func=ACT.Silu,
                )
        for g2 in range(GROUPS2):
            nc.vector.quantize_mx(
                out=h_codes[:, g2, :].bitcast(FP8X4),
                scales=h_scales[:, g2, :],
                in_=h_grouped[:, g2, :, :].rearrange("p r t -> p (r t)"),
            )

        aT_ps = [sum_pool.tile([P, ROWS], F32, name="aT_ps%d" % jt, tag="sum_%d" % jt) for jt in range(J_TILES)]
        a_ps = [sum_pool.tile([P, H1], F32, name="a_ps%d" % e, tag="sum_%d" % (J_TILES + e)) for e in range(ROW_TILES)]
        for g2 in range(GROUPS2):
            for jt in range(J_TILES):
                j_cols = slice(jt * P, (jt + 1) * P)
                nc.tensor.matmul_mx(
                    out=aT_ps[jt][:],
                    lhsT=w2_words[:, g2, j_cols].bitcast(FP8X4),
                    lhsT_scale=w2_scale_tile[:, g2, j_cols],
                    rhs=h_codes[:, g2, :].bitcast(FP8X4),
                    rhs_scale=h_scales[:, g2, :],
                    start=(g2 == 0),
                    stop=(g2 == GROUPS2 - 1),
                )
            for e in range(ROW_TILES):
                rows = slice(e * P, (e + 1) * P)
                nc.tensor.matmul_mx(
                    out=a_ps[e][:],
                    lhsT=h_codes[:, g2, rows].bitcast(FP8X4),
                    lhsT_scale=h_scales[:, g2, rows],
                    rhs=w2_words[:, g2, :].bitcast(FP8X4),
                    rhs_scale=w2_scale_tile[:, g2, :],
                    start=(g2 == 0),
                    stop=(g2 == GROUPS2 - 1),
                )

        aT = keep.tile([P, J_TILES, ROWS], F32)
        nc.scalar.copy(out=aT[:, 0, :], in_=aT_ps[0][:])
        nc.vector.tensor_copy(out=aT[:, 1, :], in_=aT_ps[1][:])
        a_sq = keep.tile([P, ROW_TILES, H1], F32)
        aa = keep.tile([P, ROW_TILES], F32)
        for e in range(ROW_TILES):
            nc.scalar.activation(out=a_sq[:, e, :], in_=a_ps[e][:], func=ACT.Square, accum_out=aa[:, e : e + 1])
        z = keep.tile([P, ROW_TILES, H1], F32)
        for e in range(ROW_TILES):
            nc.vector.tensor_tensor(out=z[:, e, :], in0=a_ps[e][:], in1=b2_rows[:], op=ALU.add)
        nc.sync.dma_start(out=out_0.rearrange("(p e) j -> p e j", e=ROW_TILES), in_=z[:])

        dots = work_pool.tile([P, ROW_TILES, CENTROIDS], F32, name="dots", tag="work")
        for e in range(ROW_TILES):
            for jt in range(J_TILES):
                nc.tensor.matmul(
                    dots[:, e, :],
                    lhsT=aT[:, jt, e * P : (e + 1) * P],
                    rhs=c_m2[:, jt, :],
                    start=(jt == 0),
                    stop=(jt == J_TILES - 1),
                )
        one_plus_d2 = keep.tile([P, ROW_TILES, CENTROIDS], F32)
        for e in range(ROW_TILES):
            nc.vector.scalar_tensor_tensor(
                out=one_plus_d2[:, e, :],
                in0=dots[:, e, :],
                scalar=aa[:, e : e + 1],
                in1=cc1[:],
                op0=ALU.add,
                op1=ALU.add,
            )
        kern = keep.tile([P, ROW_TILES, CENTROIDS], F32)
        nc.vector.reciprocal(out=kern[:], in_=one_plus_d2[:])
        kern_sum = keep.tile([P, ROW_TILES], F32)
        nc.vector.tensor_reduce(out=kern_sum[:], in_=kern[:], axis=AXIS.X, op=ALU.add)
        inv_sum = keep.tile([P, ROW_TILES], F32)
        nc.vector.reciprocal(out=inv_sum[:], in_=kern_sum[:])
        q = keep.tile([P, ROW_TILES, CENTROIDS], F32)
        nc.vector.tensor_tensor(
            out=q[:],
            in0=kern[:],
            in1=inv_sum[:].unsqueeze(2).to_broadcast([P, ROW_TILES, CENTROIDS]),
            op=ALU.mult,
        )
        nc.sync.dma_start(out=out_1.rearrange("(p e) k -> p e k", e=ROW_TILES), in_=q[:])
